import numpy as np
import ml_dtypes


def mxq(x, axis, fmt="e4m3"):
    dtype, down = {"e4m3": (ml_dtypes.float8_e4m3fn, 7), "e5m2": (ml_dtypes.float8_e5m2, 14)}[fmt]
    v = np.moveaxis(np.asarray(x, np.float32).astype(ml_dtypes.bfloat16).astype(np.float64), axis, -1)
    blocks = v.reshape(v.shape[:-1] + (-1, 32))
    amax = np.abs(blocks).max(-1, keepdims=True)
    byte = np.maximum(np.where(amax > 0, np.frexp(amax)[1] - 1 + 127, 0) - down, 1)
    scale = np.exp2(byte - 127.0)
    codes = (blocks / scale).astype(np.float32).astype(dtype).astype(np.float64)
    return np.moveaxis((codes * scale).reshape(v.shape), -1, axis)


WIDE = False


def mx_kscale(k):
    if not WIDE:
        return np.ones(k)
    levels = np.array([30, -30])
    if k % 512:
        return np.exp2(np.random.permutation(np.resize(levels, k // 32))).repeat(32)
    a = np.empty((k // 512, 16))
    for p in range(k // 512):
        a[p, :8] = np.random.permutation(np.resize(levels, 8))
        for g in range(8):
            far = levels[np.abs(levels - a[p, g]) >= 10]
            a[p, g + 8] = far[np.random.randint(len(far))]
    return np.exp2(a.ravel()).repeat(32)


BF16 = ml_dtypes.bfloat16


def bf(x):
    return np.asarray(x, np.float32).astype(BF16)


def f64(x):
    return np.asarray(x).astype(np.float64)


B, S, D_IN, D_OUT = 2, 256, 2048, 2048


def quant8(w):
    mv = np.max(np.abs(w))
    q = np.ceil(np.log2(mv)) - 6.0
    scale = np.exp2(q)
    return np.round(w / scale) * scale


def setup_inputs():
    s = mx_kscale(D_IN)
    x = np.random.standard_normal((B, S, D_IN))
    weight = np.random.standard_normal((D_OUT, D_IN)) * 3.0 / np.sqrt(D_IN)
    w_upper = quant8(weight)
    w_lower = weight - w_upper
    return {"x": bf(x * s), "weight_upper": bf(w_upper / s[None, :]), "weight_lower": bf(w_lower / s[None, :])}


def reference(x, weight_upper, weight_lower):
    xq = mxq(f64(x), 2, "e5m2")
    y_upper = xq @ mxq(f64(weight_upper), 1, "e4m3").T
    y_lower = xq @ mxq(f64(weight_lower), 1, "e4m3").T
    return y_upper + y_lower

@@ -1,0 +1,182 @@
+from contextlib import ExitStack
+
+import concourse.mybir as mybir
+from concourse.masks import make_identity
+
+F32 = mybir.dt.float32
+BF16 = mybir.dt.bfloat16
+U32 = mybir.dt.uint32
+U8 = mybir.dt.uint8
+E4M3_X4 = mybir.dt.float8_e4m3fn_x4
+E5M2_X4 = mybir.dt.float8_e5m2_x4
+
+TOKENS, D_IN, D_OUT = 512, 2048, 2048
+FLOPS = 2 * 2 * TOKENS * D_IN * D_OUT
+
+P = 128
+ROWS = 512
+K_UNIT = 1024
+W_UNIT = K_UNIT // 2
+RAW_BUFS = 10
+
+
+def tile_virtual16bmatmul_kernel(tc, x, weight_upper, weight_lower, out):
+    nc = tc.nc
+    x_flat = x.flatten_outer_dims()
+    out_flat = out.flatten_outer_dims()
+
+    units = [(x_flat, 0, 0, None, False, False)]
+    units.append((weight_upper, 0, 0, 0, True, False))
+    units.append((x_flat, 0, 1, None, False, False))
+    units.append((weight_upper, 0, 1, 0, False, False))
+    units.append((weight_lower, 0, 0, 0, False, False))
+    units.append((weight_lower, 0, 1, 0, False, True))
+    for n in range(1, D_OUT // ROWS):
+        units.append((weight_upper, n * ROWS, 0, n, True, False))
+        units.append((weight_upper, n * ROWS, 1, n, False, False))
+        units.append((weight_lower, n * ROWS, 0, n, False, False))
+        units.append((weight_lower, n * ROWS, 1, n, False, True))
+    n_units = len(units)
+
+    with ExitStack() as ctx:
+        const = ctx.enter_context(tc.tile_pool(name="const", bufs=1))
+        raw_pool = ctx.enter_context(tc.tile_pool(name="rawp", bufs=RAW_BUFS))
+        reord_pool = ctx.enter_context(tc.tile_pool(name="reordp", bufs=3))
+        grouped_pool = ctx.enter_context(tc.tile_pool(name="groupedp", bufs=4))
+        wq_pool = ctx.enter_context(tc.tile_pool(name="wqp", bufs=6))
+        res_pool = ctx.enter_context(tc.tile_pool(name="resp", bufs=6))
+        t_psum = ctx.enter_context(tc.psum_pool(name="tpsum", bufs=4))
+        acc_psum = ctx.enter_context(tc.psum_pool(name="accpsum", bufs=4))
+
+        ident = const.tile([P, P], F32, name="ident")
+        make_identity(nc, ident[:])
+        x_codes = const.tile([P, 4, TOKENS], U32, name="x_codes", align_bytes=64)
+        x_scales = const.tile([P, 4, TOKENS], U8, name="x_scales", align_bytes=64)
+        warm_in = const.tile([P, 1], F32, name="warm_in")
+        warm_out = const.tile([P, 1], F32, name="warm_out")
+
+        raw = {}
+        reord = {}
+        grouped = {}
+        quantised = {}
+        acc = {}
+
+        def load(i, pieces):
+            src, r0, h, n, first, last = units[i]
+            t = raw_pool.tile([P, 4, K_UNIT], BF16, name="raw", tag="raw")
+            raw[i] = t
+            per = 4 // pieces
+            for a in range(pieces):
+                nc.sync.dma_start(
+                    out=t[:, a * per : (a + 1) * per, :],
+                    in_=src[
+                        r0 + a * per * P : r0 + (a + 1) * per * P,
+                        h * K_UNIT : (h + 1) * K_UNIT,
+                    ].rearrange("(j p) c -> p j c", p=P),
+                )
+
+        def reorder(i, jp):
+            if jp == 0:
+                reord[i] = reord_pool.tile([P, 2, 4 * 256], F32, name="reord", tag="reord")
+            words = raw[i][:].rearrange("p j c -> p (j c)").bitcast(F32)
+            nc.vector.tensor_copy(
+                out=reord[i][:].rearrange("p u (b r) -> p u b r", r=8)[:, :, jp * 64 : (jp + 1) * 64, :],
+                in_=words.rearrange("p (b u r) -> p u b r", u=2, r=8)[:, :, jp * 64 : (jp + 1) * 64, :],
+            )
+
+        def transpose(i, jp):
+            if jp == 0:
+                grouped[i] = [
+                    grouped_pool.tile([P, ROWS, 2], F32, name="grouped", tag="grouped", align_bytes=64)
+                    for g in range(2)
+                ]
+            for g in range(2):
+                bank = t_psum.tile([P, 2, 256], F32, name="bank", tag="bank")
+                for jj in range(2):
+                    for u in range(2):
+                        c0 = (2 * jp + jj) * 256 + g * P
+                        nc.tensor.transpose(
+                            out=bank[:, u, jj * P : (jj + 1) * P],
+                            in_=reord[i][:, u, c0 : c0 + P],
+                            identity=ident[:],
+                        )
+                nc.scalar.copy(
+                    out=grouped[i][g][:, jp * 256 : (jp + 1) * 256, :],
+                    in_=bank[:].rearrange("p u r -> p r u"),
+                )
+
+        def quantise(i, g):
+            src, r0, h, n, first, last = units[i]
+            values = grouped[i][g][:].rearrange("p r u -> p (r u)").bitcast(BF16)
+            if n is None:
+                nc.vector.quantize_mx(
+                    out=x_codes[:, 2 * h + g, :].bitcast(E5M2_X4),
+                    scales=x_scales[:, 2 * h + g, :],
+                    in_=values,
+                )
+            else:
+                w_codes = wq_pool.tile([P, ROWS], U32, name="w_codes", tag="w_codes", align_bytes=64)
+                w_scales = wq_pool.tile([P, ROWS], U8, name="w_scales", tag="w_scales", align_bytes=64)
+                quantised[(i, g)] = (w_codes, w_scales)
+                nc.vector.quantize_mx(out=w_codes[:].bitcast(E4M3_X4), scales=w_scales[:], in_=values)
+
+        def one_pass(i, g, m):
+            src, r0, h, n, first, last = units[i]
+            w_codes, w_scales = quantised[(i, g)]
+            cols = slice(m * P, (m + 1) * P)
+            nc.tensor.matmul_mx(
+                out=acc[m][:],
+                lhsT=x_codes[:, 2 * h + g, cols].bitcast(E5M2_X4),
+                lhsT_scale=x_scales[:, 2 * h + g, cols],
+                rhs=w_codes[:].bitcast(E4M3_X4),
+                rhs_scale=w_scales[:],
+                start=(first and g == 0),
+                stop=(last and g == 1),
+            )
+
+        def multiply(i):
+            src, r0, h, n, first, last = units[i]
+            if n is None:
+                return
+            if first:
+                for m in range(4):
+                    acc[m] = acc_psum.tile([P, ROWS], F32, name="acc", tag="acc")
+            if not last:
+                for g in range(2):
+                    for m in range(4):
+                        one_pass(i, g, m)
+                return
+            for m in range(4):
+                for g in range(2):
+                    one_pass(i, g, m)
+                res = res_pool.tile([P, ROWS], F32, name="res", tag="res")
+                if m % 2 == 0:
+                    nc.vector.tensor_copy(out=res[:], in_=acc[m][:])
+                else:
+                    nc.scalar.copy(out=res[:], in_=acc[m][:])
+                nc.sync.dma_start(
+                    out=out_flat[m * P : (m + 1) * P, n * ROWS : (n + 1) * ROWS], in_=res[:]
+                )
+
+        with tc.manual_schedule():
+            nc.vector.memset(warm_in[:], 0.0)
+            nc.scalar.copy(out=warm_out[:], in_=warm_in[:])
+            for i in range(RAW_BUFS):
+                load(i, 4 if i < 4 else 1)
+            for i in range(2):
+                reorder(i, 0)
+                reorder(i, 1)
+            for s in range(n_units + 1):
+                if s < n_units:
+                    transpose(s, 0)
+                    transpose(s, 1)
+                    quantise(s, 0)
+                    if s + 2 < n_units:
+                        reorder(s + 2, 0)
+                    quantise(s, 1)
+                    if s + 2 < n_units:
+                        reorder(s + 2, 1)
+                    if s + RAW_BUFS < n_units:
+                        load(s + RAW_BUFS, 1)
+                if s >= 1:
+                    multiply(s - 1)

@@ -14,10 +14,13 @@ TOKENS, D_IN, D_OUT = 512, 2048, 2048
 FLOPS = 2 * 2 * TOKENS * D_IN * D_OUT
 
 P = 128
+K_PASS = 512
 ROWS = 512
-K_UNIT = 1024
-W_UNIT = K_UNIT // 2
-RAW_BUFS = 10
+HALF = 256
+K_BLOCK = 2 * K_PASS
+RAW_BUFS = 20
+N_TILES = D_OUT // ROWS
+M_TILES = TOKENS // P
 
 
 def tile_virtual16bmatmul_kernel(tc, x, weight_upper, weight_lower, out):
@@ -25,28 +28,21 @@ def tile_virtual16bmatmul_kernel(tc, x, weight_upper, weight_lower, out):
     x_flat = x.flatten_outer_dims()
     out_flat = out.flatten_outer_dims()
 
-    units = [(x_flat, 0, 0, None, False, False)]
-    units.append((weight_upper, 0, 0, 0, True, False))
-    units.append((x_flat, 0, 1, None, False, False))
-    units.append((weight_upper, 0, 1, 0, False, False))
-    units.append((weight_lower, 0, 0, 0, False, False))
-    units.append((weight_lower, 0, 1, 0, False, True))
-    for n in range(1, D_OUT // ROWS):
-        units.append((weight_upper, n * ROWS, 0, n, True, False))
-        units.append((weight_upper, n * ROWS, 1, n, False, False))
-        units.append((weight_lower, n * ROWS, 0, n, False, False))
-        units.append((weight_lower, n * ROWS, 1, n, False, True))
-    n_units = len(units)
+    blocks = [(x_flat, 0, 0), (weight_upper, 0, 0), (x_flat, 0, 1), (weight_upper, 0, 1)]
+    blocks += [(weight_lower, 0, 0), (weight_lower, 0, 1)]
+    for n in range(1, N_TILES):
+        blocks += [(weight_upper, n, 0), (weight_upper, n, 1), (weight_lower, n, 0), (weight_lower, n, 1)]
+    n_blocks = len(blocks)
 
     with ExitStack() as ctx:
         const = ctx.enter_context(tc.tile_pool(name="const", bufs=1))
-        raw_pool = ctx.enter_context(tc.tile_pool(name="rawp", bufs=RAW_BUFS))
-        reord_pool = ctx.enter_context(tc.tile_pool(name="reordp", bufs=3))
-        grouped_pool = ctx.enter_context(tc.tile_pool(name="groupedp", bufs=4))
-        wq_pool = ctx.enter_context(tc.tile_pool(name="wqp", bufs=6))
-        res_pool = ctx.enter_context(tc.tile_pool(name="resp", bufs=6))
-        t_psum = ctx.enter_context(tc.psum_pool(name="tpsum", bufs=4))
-        acc_psum = ctx.enter_context(tc.psum_pool(name="accpsum", bufs=4))
+        raw_pool = ctx.enter_context(tc.tile_pool(name="raw_pool", bufs=RAW_BUFS))
+        reord_pool = ctx.enter_context(tc.tile_pool(name="reord_pool", bufs=4))
+        grouped_pool = ctx.enter_context(tc.tile_pool(name="grouped_pool", bufs=4))
+        wq_pool = ctx.enter_context(tc.tile_pool(name="wq_pool", bufs=6))
+        res_pool = ctx.enter_context(tc.tile_pool(name="res_pool", bufs=N_TILES * M_TILES))
+        t_psum = ctx.enter_context(tc.psum_pool(name="t_psum", bufs=4))
+        acc_psum = ctx.enter_context(tc.psum_pool(name="acc_psum", bufs=M_TILES))
 
         ident = const.tile([P, P], F32, name="ident")
         make_identity(nc, ident[:])
@@ -58,125 +54,112 @@ def tile_virtual16bmatmul_kernel(tc, x, weight_upper, weight_lower, out):
         raw = {}
         reord = {}
         grouped = {}
-        quantised = {}
+        w_quantised = {}
         acc = {}
 
-        def load(i, pieces):
-            src, r0, h, n, first, last = units[i]
-            t = raw_pool.tile([P, 4, K_UNIT], BF16, name="raw", tag="raw")
-            raw[i] = t
-            per = 4 // pieces
-            for a in range(pieces):
-                nc.sync.dma_start(
-                    out=t[:, a * per : (a + 1) * per, :],
-                    in_=src[
-                        r0 + a * per * P : r0 + (a + 1) * per * P,
-                        h * K_UNIT : (h + 1) * K_UNIT,
-                    ].rearrange("(j p) c -> p j c", p=P),
-                )
-
-        def reorder(i, jp):
-            if jp == 0:
-                reord[i] = reord_pool.tile([P, 2, 4 * 256], F32, name="reord", tag="reord")
-            words = raw[i][:].rearrange("p j c -> p (j c)").bitcast(F32)
-            nc.vector.tensor_copy(
-                out=reord[i][:].rearrange("p u (b r) -> p u b r", r=8)[:, :, jp * 64 : (jp + 1) * 64, :],
-                in_=words.rearrange("p (b u r) -> p u b r", u=2, r=8)[:, :, jp * 64 : (jp + 1) * 64, :],
+        def load(k):
+            src, n, h = blocks[k // 2]
+            r0 = n * ROWS + (k % 2) * HALF
+            raw[k] = raw_pool.tile([P, 2, K_BLOCK], BF16, name="raw", tag="raw")
+            nc.sync.dma_start(
+                out=raw[k][:],
+                in_=src[r0 : r0 + HALF, h * K_BLOCK : (h + 1) * K_BLOCK].rearrange("(j p) c -> p j c", p=P),
             )
 
-        def transpose(i, jp):
-            if jp == 0:
-                grouped[i] = [
+        def reorder(k):
+            reord[k] = reord_pool.tile([P, 2, K_BLOCK // 2], F32, name="reord", tag="reord")
+            words = raw[k][:].rearrange("p j c -> p (j c)").bitcast(F32)
+            nc.vector.tensor_copy(
+                out=reord[k][:].rearrange("p u (b r) -> p u b r", r=8),
+                in_=words.rearrange("p (b u r) -> p u b r", u=2, r=8),
+            )
+            if k + RAW_BUFS < 2 * n_blocks:
+                load(k + RAW_BUFS)
+
+        def transpose(k):
+            s = k // 2
+            if k % 2 == 0:
+                grouped[s] = [
                     grouped_pool.tile([P, ROWS, 2], F32, name="grouped", tag="grouped", align_bytes=64)
                     for g in range(2)
                 ]
             for g in range(2):
-                bank = t_psum.tile([P, 2, 256], F32, name="bank", tag="bank")
-                for jj in range(2):
+                bank = t_psum.tile([P, 2, HALF], F32, name="bank", tag="bank")
+                for j in range(2):
                     for u in range(2):
-                        c0 = (2 * jp + jj) * 256 + g * P
+                        c0 = (2 * j + g) * P
                         nc.tensor.transpose(
-                            out=bank[:, u, jj * P : (jj + 1) * P],
-                            in_=reord[i][:, u, c0 : c0 + P],
-                            identity=ident[:],
+                            out=bank[:, u, j * P : (j + 1) * P], in_=reord[k][:, u, c0 : c0 + P], identity=ident[:]
                         )
                 nc.scalar.copy(
-                    out=grouped[i][g][:, jp * 256 : (jp + 1) * 256, :],
+                    out=grouped[s][g][:, (k % 2) * HALF : (k % 2 + 1) * HALF, :],
                     in_=bank[:].rearrange("p u r -> p r u"),
                 )
 
-        def quantise(i, g):
-            src, r0, h, n, first, last = units[i]
-            values = grouped[i][g][:].rearrange("p r u -> p (r u)").bitcast(BF16)
-            if n is None:
+        def quantise(s, g):
+            src, n, h = blocks[s]
+            values = grouped[s][g][:].rearrange("p r u -> p (r u)").bitcast(BF16)
+            if src is x_flat:
                 nc.vector.quantize_mx(
-                    out=x_codes[:, 2 * h + g, :].bitcast(E5M2_X4),
-                    scales=x_scales[:, 2 * h + g, :],
-                    in_=values,
+                    out=x_codes[:, 2 * h + g, :].bitcast(E5M2_X4), scales=x_scales[:, 2 * h + g, :], in_=values
                 )
             else:
                 w_codes = wq_pool.tile([P, ROWS], U32, name="w_codes", tag="w_codes", align_bytes=64)
                 w_scales = wq_pool.tile([P, ROWS], U8, name="w_scales", tag="w_scales", align_bytes=64)
-                quantised[(i, g)] = (w_codes, w_scales)
+                w_quantised[(s, g)] = (w_codes, w_scales)
                 nc.vector.quantize_mx(out=w_codes[:].bitcast(E4M3_X4), scales=w_scales[:], in_=values)
 
-        def one_pass(i, g, m):
-            src, r0, h, n, first, last = units[i]
-            w_codes, w_scales = quantised[(i, g)]
-            cols = slice(m * P, (m + 1) * P)
+        def one_pass(s, g, m):
+            src, n, h = blocks[s]
+            w_codes, w_scales = w_quantised[(s, g)]
+            tokens = slice(m * P, (m + 1) * P)
             nc.tensor.matmul_mx(
                 out=acc[m][:],
-                lhsT=x_codes[:, 2 * h + g, cols].bitcast(E5M2_X4),
-                lhsT_scale=x_scales[:, 2 * h + g, cols],
+                lhsT=x_codes[:, 2 * h + g, tokens].bitcast(E5M2_X4),
+                lhsT_scale=x_scales[:, 2 * h + g, tokens],
                 rhs=w_codes[:].bitcast(E4M3_X4),
                 rhs_scale=w_scales[:],
-                start=(first and g == 0),
-                stop=(last and g == 1),
+                start=(src is weight_upper and h == 0 and g == 0),
+                stop=(src is weight_lower and h == 1 and g == 1),
             )
 
-        def multiply(i):
-            src, r0, h, n, first, last = units[i]
-            if n is None:
+        def multiply(s):
+            src, n, h = blocks[s]
+            if src is x_flat:
                 return
-            if first:
-                for m in range(4):
+            if src is weight_upper and h == 0:
+                for m in range(M_TILES):
                     acc[m] = acc_psum.tile([P, ROWS], F32, name="acc", tag="acc")
-            if not last:
+            if not (src is weight_lower and h == 1):
                 for g in range(2):
-                    for m in range(4):
-                        one_pass(i, g, m)
+                    for m in range(M_TILES):
+                        one_pass(s, g, m)
                 return
-            for m in range(4):
+            for m in range(M_TILES):
                 for g in range(2):
-                    one_pass(i, g, m)
+                    one_pass(s, g, m)
                 res = res_pool.tile([P, ROWS], F32, name="res", tag="res")
                 if m % 2 == 0:
                     nc.vector.tensor_copy(out=res[:], in_=acc[m][:])
                 else:
                     nc.scalar.copy(out=res[:], in_=acc[m][:])
-                nc.sync.dma_start(
-                    out=out_flat[m * P : (m + 1) * P, n * ROWS : (n + 1) * ROWS], in_=res[:]
-                )
+                nc.sync.dma_start(out=out_flat[m * P : (m + 1) * P, n * ROWS : (n + 1) * ROWS], in_=res[:])
 
         with tc.manual_schedule():
             nc.vector.memset(warm_in[:], 0.0)
             nc.scalar.copy(out=warm_out[:], in_=warm_in[:])
-            for i in range(RAW_BUFS):
-                load(i, 4 if i < 4 else 1)
-            for i in range(2):
-                reorder(i, 0)
-                reorder(i, 1)
-            for s in range(n_units + 1):
-                if s < n_units:
-                    transpose(s, 0)
-                    transpose(s, 1)
+            for k in range(RAW_BUFS):
+                load(k)
+            reorder(0)
+            reorder(1)
+            for s in range(n_blocks + 1):
+                if s < n_blocks:
+                    transpose(2 * s)
+                    transpose(2 * s + 1)
+                    if s + 1 < n_blocks:
+                        reorder(2 * s + 2)
+                        reorder(2 * s + 3)
                     quantise(s, 0)
-                    if s + 2 < n_units:
-                        reorder(s + 2, 0)
                     quantise(s, 1)
-                    if s + 2 < n_units:
-                        reorder(s + 2, 1)
-                    if s + RAW_BUFS < n_units:
-                        load(s + RAW_BUFS, 1)
                 if s >= 1:
                     multiply(s - 1)

@@ -19,6 +19,8 @@ ROWS = 512
 HALF = 256
 K_BLOCK = 2 * K_PASS
 RAW_BUFS = 20
+WARM_START = 7
+WARM_BETWEEN = 2
 N_TILES = D_OUT // ROWS
 M_TILES = TOKENS // P
 
@@ -50,12 +52,17 @@ def tile_virtual16bmatmul_kernel(tc, x, weight_upper, weight_lower, out):
         x_scales = const.tile([P, 4, TOKENS], U8, name="x_scales", align_bytes=64)
         warm_in = const.tile([P, 1], F32, name="warm_in")
         warm_out = const.tile([P, 1], F32, name="warm_out")
+        zeros = const.tile([P, ROWS], BF16, name="zeros")
 
         raw = {}
         reord = {}
         grouped = {}
         w_quantised = {}
         acc = {}
+
+        def keep_warm(count):
+            for i in range(count):
+                nc.tensor.matmul(out=idle_bank[:], lhsT=zeros[:, 0:P], rhs=zeros[:], start=True, stop=True)
 
         def load(k):
             src, n, h = blocks[k // 2]
@@ -146,16 +153,23 @@ def tile_virtual16bmatmul_kernel(tc, x, weight_upper, weight_lower, out):
                 nc.sync.dma_start(out=out_flat[m * P : (m + 1) * P, n * ROWS : (n + 1) * ROWS], in_=res[:])
 
         with tc.manual_schedule():
+            nc.vector.memset(zeros[:], 0.0)
             nc.vector.memset(warm_in[:], 0.0)
             nc.scalar.copy(out=warm_out[:], in_=warm_in[:])
             for k in range(RAW_BUFS):
                 load(k)
+            idle_bank = acc_psum.tile([P, ROWS], F32, name="acc", tag="acc")
+            keep_warm(WARM_START)
             reorder(0)
             reorder(1)
             for s in range(n_blocks + 1):
                 if s < n_blocks:
                     transpose(2 * s)
+                    if s < 2:
+                        keep_warm(WARM_BETWEEN)
                     transpose(2 * s + 1)
+                    if s < 2:
+                        keep_warm(WARM_BETWEEN)
                     if s + 1 < n_blocks:
                         reorder(2 * s + 2)
                         reorder(2 * s + 3)

@@ -18,11 +18,11 @@ K_PASS = 512
 ROWS = 512
 HALF = 256
 K_BLOCK = 2 * K_PASS
-RAW_BUFS = 20
-WARM_START = 7
-WARM_BETWEEN = 2
 N_TILES = D_OUT // ROWS
 M_TILES = TOKENS // P
+PASSES = 2 * D_IN // K_PASS
+RAW_BUFS = 16
+FIRST_SWEEP = 3
 
 
 def tile_virtual16bmatmul_kernel(tc, x, weight_upper, weight_lower, out):
@@ -34,17 +34,17 @@ def tile_virtual16bmatmul_kernel(tc, x, weight_upper, weight_lower, out):
     blocks += [(weight_lower, 0, 0), (weight_lower, 0, 1)]
     for n in range(1, N_TILES):
         blocks += [(weight_upper, n, 0), (weight_upper, n, 1), (weight_lower, n, 0), (weight_lower, n, 1)]
-    n_blocks = len(blocks)
+    n_halves = 2 * len(blocks)
+    head = 7
 
     with ExitStack() as ctx:
         const = ctx.enter_context(tc.tile_pool(name="const", bufs=1))
         raw_pool = ctx.enter_context(tc.tile_pool(name="raw_pool", bufs=RAW_BUFS))
-        reord_pool = ctx.enter_context(tc.tile_pool(name="reord_pool", bufs=4))
+        reord_pool = ctx.enter_context(tc.tile_pool(name="reord_pool", bufs=8))
         grouped_pool = ctx.enter_context(tc.tile_pool(name="grouped_pool", bufs=4))
-        wq_pool = ctx.enter_context(tc.tile_pool(name="wq_pool", bufs=6))
+        wq_pool = ctx.enter_context(tc.tile_pool(name="wq_pool", bufs=10))
         res_pool = ctx.enter_context(tc.tile_pool(name="res_pool", bufs=N_TILES * M_TILES))
-        t_psum = ctx.enter_context(tc.psum_pool(name="t_psum", bufs=4))
-        acc_psum = ctx.enter_context(tc.psum_pool(name="acc_psum", bufs=M_TILES))
+        psum = ctx.enter_context(tc.psum_pool(name="psum", bufs=1))
 
         ident = const.tile([P, P], F32, name="ident")
         make_identity(nc, ident[:])
@@ -52,17 +52,23 @@ def tile_virtual16bmatmul_kernel(tc, x, weight_upper, weight_lower, out):
         x_scales = const.tile([P, 4, TOKENS], U8, name="x_scales", align_bytes=64)
         warm_in = const.tile([P, 1], F32, name="warm_in")
         warm_out = const.tile([P, 1], F32, name="warm_out")
-        zeros = const.tile([P, ROWS], BF16, name="zeros")
 
         raw = {}
         reord = {}
         grouped = {}
         w_quantised = {}
         acc = {}
+        passes_done = {}
+        rotation = {"banks": [4, 5, 6, 7], "taken": 0}
 
-        def keep_warm(count):
-            for i in range(count):
-                nc.tensor.matmul(out=idle_bank[:], lhsT=zeros[:, 0:P], rhs=zeros[:], start=True, stop=True)
+        def bank_tile(b):
+            return psum.tile([P, 2, HALF], F32, name="bank%d" % b, tag="bank%d" % b)
+
+        def next_bank():
+            banks = rotation["banks"]
+            b = banks[rotation["taken"] % len(banks)]
+            rotation["taken"] += 1
+            return bank_tile(b)
 
         def load(k):
             src, n, h = blocks[k // 2]
@@ -80,28 +86,29 @@ def tile_virtual16bmatmul_kernel(tc, x, weight_upper, weight_lower, out):
                 out=reord[k][:].rearrange("p u (b r) -> p u b r", r=8),
                 in_=words.rearrange("p (b u r) -> p u b r", u=2, r=8),
             )
-            if k + RAW_BUFS < 2 * n_blocks:
+            if k + RAW_BUFS < n_halves:
                 load(k + RAW_BUFS)
 
-        def transpose(k):
-            s = k // 2
-            if k % 2 == 0:
-                grouped[s] = [
-                    grouped_pool.tile([P, ROWS, 2], F32, name="grouped", tag="grouped", align_bytes=64)
-                    for g in range(2)
-                ]
-            for g in range(2):
-                bank = t_psum.tile([P, 2, HALF], F32, name="bank", tag="bank")
-                for j in range(2):
-                    for u in range(2):
-                        c0 = (2 * j + g) * P
-                        nc.tensor.transpose(
-                            out=bank[:, u, j * P : (j + 1) * P], in_=reord[k][:, u, c0 : c0 + P], identity=ident[:]
-                        )
-                nc.scalar.copy(
-                    out=grouped[s][g][:, (k % 2) * HALF : (k % 2 + 1) * HALF, :],
-                    in_=bank[:].rearrange("p u r -> p r u"),
-                )
+        def transpose(s):
+            grouped[s] = [
+                grouped_pool.tile([P, ROWS, 2], F32, name="grouped", tag="grouped", align_bytes=64)
+                for g in range(2)
+            ]
+            for a in range(2):
+                for g in range(2):
+                    bank = next_bank()
+                    for j in range(2):
+                        for u in range(2):
+                            c0 = (2 * j + g) * P
+                            nc.tensor.transpose(
+                                out=bank[:, u, j * P : (j + 1) * P],
+                                in_=reord[2 * s + a][:, u, c0 : c0 + P],
+                                identity=ident[:],
+                            )
+                    nc.scalar.copy(
+                        out=grouped[s][g][:, a * HALF : (a + 1) * HALF, :],
+                        in_=bank[:].rearrange("p u r -> p r u"),
+                    )
 
         def quantise(s, g):
             src, n, h = blocks[s]
@@ -118,62 +125,77 @@ def tile_virtual16bmatmul_kernel(tc, x, weight_upper, weight_lower, out):
 
         def one_pass(s, g, m):
             src, n, h = blocks[s]
+            done = passes_done.get((n, m), 0)
+            passes_done[(n, m)] = done + 1
+            if done == 0:
+                acc[m] = bank_tile(m) if n == 0 else next_bank()
             w_codes, w_scales = w_quantised[(s, g)]
             tokens = slice(m * P, (m + 1) * P)
+            sums = acc[m][:].rearrange("p a b -> p (a b)")
             nc.tensor.matmul_mx(
-                out=acc[m][:],
+                out=sums,
                 lhsT=x_codes[:, 2 * h + g, tokens].bitcast(E5M2_X4),
                 lhsT_scale=x_scales[:, 2 * h + g, tokens],
                 rhs=w_codes[:].bitcast(E4M3_X4),
                 rhs_scale=w_scales[:],
-                start=(src is weight_upper and h == 0 and g == 0),
-                stop=(src is weight_lower and h == 1 and g == 1),
+                start=(done == 0),
+                stop=(done == PASSES - 1),
             )
-
-        def multiply(s):
-            src, n, h = blocks[s]
-            if src is x_flat:
-                return
-            if src is weight_upper and h == 0:
-                for m in range(M_TILES):
-                    acc[m] = acc_psum.tile([P, ROWS], F32, name="acc", tag="acc")
-            if not (src is weight_lower and h == 1):
-                for g in range(2):
-                    for m in range(M_TILES):
-                        one_pass(s, g, m)
-                return
-            for m in range(M_TILES):
-                for g in range(2):
-                    one_pass(s, g, m)
+            if done == PASSES - 1:
                 res = res_pool.tile([P, ROWS], F32, name="res", tag="res")
-                if m % 2 == 0:
-                    nc.vector.tensor_copy(out=res[:], in_=acc[m][:])
+                if n > 0 and m % 2 == 1:
+                    nc.vector.tensor_copy(out=res[:], in_=sums)
                 else:
-                    nc.scalar.copy(out=res[:], in_=acc[m][:])
+                    nc.scalar.copy(out=res[:], in_=sums)
                 nc.sync.dma_start(out=out_flat[m * P : (m + 1) * P, n * ROWS : (n + 1) * ROWS], in_=res[:])
 
         with tc.manual_schedule():
-            nc.vector.memset(zeros[:], 0.0)
             nc.vector.memset(warm_in[:], 0.0)
             nc.scalar.copy(out=warm_out[:], in_=warm_in[:])
             for k in range(RAW_BUFS):
                 load(k)
-            idle_bank = acc_psum.tile([P, ROWS], F32, name="acc", tag="acc")
-            keep_warm(WARM_START)
             reorder(0)
             reorder(1)
-            for s in range(n_blocks + 1):
-                if s < n_blocks:
-                    transpose(2 * s)
-                    if s < 2:
-                        keep_warm(WARM_BETWEEN)
-                    transpose(2 * s + 1)
-                    if s < 2:
-                        keep_warm(WARM_BETWEEN)
-                    if s + 1 < n_blocks:
-                        reorder(2 * s + 2)
-                        reorder(2 * s + 3)
-                    quantise(s, 0)
-                    quantise(s, 1)
-                if s >= 1:
-                    multiply(s - 1)
+            for s in range(head):
+                transpose(s)
+                reorder(2 * s + 2)
+                reorder(2 * s + 3)
+                quantise(s, 0)
+                quantise(s, 1)
+                if s == 0 or blocks[s - 1][0] is x_flat:
+                    continue
+                if s < head - 1:
+                    for g in range(2):
+                        for m in range(M_TILES):
+                            one_pass(s - 1, g, m)
+                else:
+                    for m in range(M_TILES):
+                        for g in range(2):
+                            one_pass(s - 1, g, m)
+
+            rotation["banks"] = [4, 5, 6, 7, 0, 1, 2, 3]
+            rotation["taken"] = 0
+            for k in range(2 * head + 2, 2 * head + 6):
+                reorder(k)
+            for n in range(1, N_TILES):
+                mine = [4 * n + 2 + i for i in range(4)]
+                ahead = [2 * (mine[0] + 4) + i for i in range(8)] if n + 1 < N_TILES else []
+                sent = 0
+                for s in mine:
+                    if s < head:
+                        continue
+                    transpose(s)
+                    for g in range(2):
+                        quantise(s, g)
+                        if sent < len(ahead):
+                            reorder(ahead[sent])
+                            sent += 1
+                for k in ahead[sent:]:
+                    reorder(k)
+                pieces = [(s, g) for s in mine for g in range(2)]
+                for m in range(M_TILES):
+                    for (s, g) in pieces[: FIRST_SWEEP + m]:
+                        one_pass(s, g, m)
+                for m in range(M_TILES):
+                    for (s, g) in pieces[FIRST_SWEEP + m :]:
+                        one_pass(s, g, m)

@@ -21,7 +21,9 @@ K_BLOCK = 2 * K_PASS
 N_TILES = D_OUT // ROWS
 M_TILES = TOKENS // P
 PASSES = 2 * D_IN // K_PASS
+
 RAW_BUFS = 16
+HEAD_PASSES = (0, 0, 1, 1, 2, 2, 2)
 FIRST_SWEEP = 3
 
 
@@ -35,7 +37,7 @@ def tile_virtual16bmatmul_kernel(tc, x, weight_upper, weight_lower, out):
     for n in range(1, N_TILES):
         blocks += [(weight_upper, n, 0), (weight_upper, n, 1), (weight_lower, n, 0), (weight_lower, n, 1)]
     n_halves = 2 * len(blocks)
-    head = 7
+    head = len(HEAD_PASSES)
 
     with ExitStack() as ctx:
         const = ctx.enter_context(tc.tile_pool(name="const", bufs=1))
@@ -89,7 +91,7 @@ def tile_virtual16bmatmul_kernel(tc, x, weight_upper, weight_lower, out):
             if k + RAW_BUFS < n_halves:
                 load(k + RAW_BUFS)
 
-        def transpose(s):
+        def transpose(s, vector_helps):
             grouped[s] = [
                 grouped_pool.tile([P, ROWS, 2], F32, name="grouped", tag="grouped", align_bytes=64)
                 for g in range(2)
@@ -105,7 +107,8 @@ def tile_virtual16bmatmul_kernel(tc, x, weight_upper, weight_lower, out):
                                 in_=reord[2 * s + a][:, u, c0 : c0 + P],
                                 identity=ident[:],
                             )
-                    nc.scalar.copy(
+                    empty = nc.vector.tensor_copy if (vector_helps and a == 1 and g == 1) else nc.scalar.copy
+                    empty(
                         out=grouped[s][g][:, a * HALF : (a + 1) * HALF, :],
                         in_=bank[:].rearrange("p u r -> p r u"),
                     )
@@ -156,22 +159,25 @@ def tile_virtual16bmatmul_kernel(tc, x, weight_upper, weight_lower, out):
                 load(k)
             reorder(0)
             reorder(1)
+
+            head_passes = [(b, g) for b in range(head - 1) if blocks[b][0] is not x_flat for g in range(2)]
+            sent = 0
             for s in range(head):
-                transpose(s)
+                transpose(s, False)
                 reorder(2 * s + 2)
                 reorder(2 * s + 3)
                 quantise(s, 0)
                 quantise(s, 1)
-                if s == 0 or blocks[s - 1][0] is x_flat:
-                    continue
-                if s < head - 1:
-                    for g in range(2):
+                now = head_passes[sent : sent + HEAD_PASSES[s]]
+                sent += HEAD_PASSES[s]
+                if sent < len(head_passes):
+                    for (b, g) in now:
                         for m in range(M_TILES):
-                            one_pass(s - 1, g, m)
+                            one_pass(b, g, m)
                 else:
                     for m in range(M_TILES):
-                        for g in range(2):
-                            one_pass(s - 1, g, m)
+                        for (b, g) in now:
+                            one_pass(b, g, m)
 
             rotation["banks"] = [4, 5, 6, 7, 0, 1, 2, 3]
             rotation["taken"] = 0
@@ -179,19 +185,15 @@ def tile_virtual16bmatmul_kernel(tc, x, weight_upper, weight_lower, out):
                 reorder(k)
             for n in range(1, N_TILES):
                 mine = [4 * n + 2 + i for i in range(4)]
-                ahead = [2 * (mine[0] + 4) + i for i in range(8)] if n + 1 < N_TILES else []
-                sent = 0
                 for s in mine:
                     if s < head:
                         continue
-                    transpose(s)
-                    for g in range(2):
-                        quantise(s, g)
-                        if sent < len(ahead):
-                            reorder(ahead[sent])
-                            sent += 1
-                for k in ahead[sent:]:
-                    reorder(k)
+                    transpose(s, True)
+                    quantise(s, 0)
+                    quantise(s, 1)
+                if n + 1 < N_TILES:
+                    for k in range(2 * (mine[0] + 4), 2 * (mine[0] + 8)):
+                        reorder(k)
                 pieces = [(s, g) for s in mine for g in range(2)]
                 for m in range(M_TILES):
                     for (s, g) in pieces[: FIRST_SWEEP + m]:

@@ -23,6 +23,7 @@ M_TILES = TOKENS // P
 PASSES = 2 * D_IN // K_PASS
 
 RAW_BUFS = 16
+FIRST_WHOLE_BLOCK = 6
 HEAD_PASSES = (0, 0, 1, 1, 2, 2, 2)
 FIRST_SWEEP = 3
 
@@ -41,7 +42,8 @@ def tile_virtual16bmatmul_kernel(tc, x, weight_upper, weight_lower, out):
 
     with ExitStack() as ctx:
         const = ctx.enter_context(tc.tile_pool(name="const", bufs=1))
-        raw_pool = ctx.enter_context(tc.tile_pool(name="raw_pool", bufs=RAW_BUFS))
+        raw_pool = ctx.enter_context(tc.tile_pool(name="raw_pool", bufs=2 * FIRST_WHOLE_BLOCK))
+        whole_pool = ctx.enter_context(tc.tile_pool(name="whole_pool", bufs=RAW_BUFS // 2))
         reord_pool = ctx.enter_context(tc.tile_pool(name="reord_pool", bufs=8))
         grouped_pool = ctx.enter_context(tc.tile_pool(name="grouped_pool", bufs=4))
         wq_pool = ctx.enter_context(tc.tile_pool(name="wq_pool", bufs=10))
@@ -74,16 +76,29 @@ def tile_virtual16bmatmul_kernel(tc, x, weight_upper, weight_lower, out):
 
         def load(k):
             src, n, h = blocks[k // 2]
+            if k // 2 >= FIRST_WHOLE_BLOCK:
+                if k % 2 == 1:
+                    whole = whole_pool.tile([P, 4, K_BLOCK], BF16, name="whole", tag="whole")
+                    raw[k - 1] = whole[:, 0:2, :]
+                    raw[k] = whole[:, 2:4, :]
+                    nc.sync.dma_start(
+                        out=whole[:],
+                        in_=src[n * ROWS : (n + 1) * ROWS, h * K_BLOCK : (h + 1) * K_BLOCK].rearrange(
+                            "(j p) c -> p j c", p=P
+                        ),
+                    )
+                return
             r0 = n * ROWS + (k % 2) * HALF
-            raw[k] = raw_pool.tile([P, 2, K_BLOCK], BF16, name="raw", tag="raw")
+            half = raw_pool.tile([P, 2, K_BLOCK], BF16, name="raw", tag="raw")
+            raw[k] = half[:]
             nc.sync.dma_start(
-                out=raw[k][:],
+                out=half[:],
                 in_=src[r0 : r0 + HALF, h * K_BLOCK : (h + 1) * K_BLOCK].rearrange("(j p) c -> p j c", p=P),
             )
 
         def reorder(k):
             reord[k] = reord_pool.tile([P, 2, K_BLOCK // 2], F32, name="reord", tag="reord")
-            words = raw[k][:].rearrange("p j c -> p (j c)").bitcast(F32)
+            words = raw[k].rearrange("p j c -> p (j c)").bitcast(F32)
             nc.vector.tensor_copy(
                 out=reord[k][:].rearrange("p u (b r) -> p u b r", r=8),
                 in_=words.rearrange("p (b u r) -> p u b r", u=2, r=8),

@@ -64,6 +64,7 @@ def tile_virtual16bmatmul_kernel(tc, x, weight_upper, weight_lower, out):
         acc = {}
         passes_done = {}
         rotation = {"banks": [4, 5, 6, 7], "taken": 0}
+        late_stores = []
 
         def bank_tile(b):
             return psum.tile([P, 2, HALF], F32, name="bank%d" % b, tag="bank%d" % b)
@@ -161,11 +162,14 @@ def tile_virtual16bmatmul_kernel(tc, x, weight_upper, weight_lower, out):
             )
             if done == PASSES - 1:
                 res = res_pool.tile([P, ROWS], F32, name="res", tag="res")
-                if n > 0 and m % 2 == 1:
+                if n in (1, 3) and m % 2 == 1:
                     nc.vector.tensor_copy(out=res[:], in_=sums)
                 else:
                     nc.scalar.copy(out=res[:], in_=sums)
-                nc.sync.dma_start(out=out_flat[m * P : (m + 1) * P, n * ROWS : (n + 1) * ROWS], in_=res[:])
+                if n == 0:
+                    late_stores.append((m, res))
+                else:
+                    nc.sync.dma_start(out=out_flat[m * P : (m + 1) * P, n * ROWS : (n + 1) * ROWS], in_=res[:])
 
         with tc.manual_schedule():
             nc.vector.memset(warm_in[:], 0.0)
@@ -198,6 +202,8 @@ def tile_virtual16bmatmul_kernel(tc, x, weight_upper, weight_lower, out):
             rotation["taken"] = 0
             for k in range(2 * head + 2, 2 * head + 6):
                 reorder(k)
+            for (m, res) in late_stores:
+                nc.sync.dma_start(out=out_flat[m * P : (m + 1) * P, 0:ROWS], in_=res[:])
             for n in range(1, N_TILES):
                 mine = [4 * n + 2 + i for i in range(4)]
                 for s in mine:

@@ -26,6 +26,7 @@ RAW_BUFS = 16
 FIRST_WHOLE_BLOCK = 6
 HEAD_PASSES = (0, 0, 1, 1, 2, 2, 2)
 FIRST_SWEEP = 3
+KEEP_WARM = 3
 
 
 def tile_virtual16bmatmul_kernel(tc, x, weight_upper, weight_lower, out):
@@ -56,6 +57,9 @@ def tile_virtual16bmatmul_kernel(tc, x, weight_upper, weight_lower, out):
         x_scales = const.tile([P, 4, TOKENS], U8, name="x_scales", align_bytes=64)
         warm_in = const.tile([P, 1], F32, name="warm_in")
         warm_out = const.tile([P, 1], F32, name="warm_out")
+        zero_l = const.tile([P, P], BF16, name="zero_l")
+        zero_r = const.tile([P, ROWS], BF16, name="zero_r")
+        warm_banks = {}
 
         raw = {}
         reord = {}
@@ -147,7 +151,10 @@ def tile_virtual16bmatmul_kernel(tc, x, weight_upper, weight_lower, out):
             done = passes_done.get((n, m), 0)
             passes_done[(n, m)] = done + 1
             if done == 0:
-                acc[m] = bank_tile(m) if n == 0 else next_bank()
+                if n == 0:
+                    acc[m] = warm_banks[m] if m in warm_banks else bank_tile(m)
+                else:
+                    acc[m] = next_bank()
             w_codes, w_scales = w_quantised[(s, g)]
             tokens = slice(m * P, (m + 1) * P)
             sums = acc[m][:].rearrange("p a b -> p (a b)")
@@ -173,6 +180,8 @@ def tile_virtual16bmatmul_kernel(tc, x, weight_upper, weight_lower, out):
 
         with tc.manual_schedule():
             nc.vector.memset(warm_in[:], 0.0)
+            nc.vector.memset(zero_l[:], 0.0)
+            nc.vector.memset(zero_r[:], 0.0)
             nc.scalar.copy(out=warm_out[:], in_=warm_in[:])
             for k in range(RAW_BUFS):
                 load(k)
@@ -183,6 +192,16 @@ def tile_virtual16bmatmul_kernel(tc, x, weight_upper, weight_lower, out):
             sent = 0
             for s in range(head):
                 transpose(s, False)
+                if s == 1:
+                    for i in range(KEEP_WARM):
+                        warm_banks[i] = bank_tile(i)
+                        nc.tensor.matmul(
+                            out=warm_banks[i][:].rearrange("p a b -> p (a b)"),
+                            lhsT=zero_l[:],
+                            rhs=zero_r[:],
+                            start=True,
+                            stop=True,
+                        )
                 reorder(2 * s + 2)
                 reorder(2 * s + 3)
                 quantise(s, 0)

@@ -169,12 +169,15 @@ def tile_virtual16bmatmul_kernel(tc, x, weight_upper, weight_lower, out):
             )
             if done == PASSES - 1:
                 res = res_pool.tile([P, ROWS], F32, name="res", tag="res")
-                if n in (1, 3) and m % 2 == 1:
+                last_n = n == N_TILES - 1
+                if (n == 1 and m % 2 == 1) or (last_n and m % 2 == 0):
                     nc.vector.tensor_copy(out=res[:], in_=sums)
                 else:
                     nc.scalar.copy(out=res[:], in_=sums)
                 if n == 0:
                     late_stores.append((m, res))
+                elif last_n and m % 2 == 1:
+                    nc.scalar.dma_start(out=out_flat[m * P : (m + 1) * P, n * ROWS : (n + 1) * ROWS], in_=res[:])
                 else:
                     nc.sync.dma_start(out=out_flat[m * P : (m + 1) * P, n * ROWS : (n + 1) * ROWS], in_=res[:])
 

@@ -24,6 +24,7 @@ PASSES = 2 * D_IN // K_PASS
 
 RAW_BUFS = 16
 FIRST_WHOLE_BLOCK = 6
+FIRST_ROWS_BLOCK = 10
 HEAD_PASSES = (0, 0, 1, 1, 2, 2, 2)
 FIRST_SWEEP = 3
 KEEP_WARM = 3
@@ -81,6 +82,15 @@ def tile_virtual16bmatmul_kernel(tc, x, weight_upper, weight_lower, out):
 
         def load(k):
             src, n, h = blocks[k // 2]
+            if k // 2 >= FIRST_ROWS_BLOCK:
+                if k % 2 == 1:
+                    rows = whole_pool.tile([P, 2, D_IN], BF16, name="whole", tag="whole")
+                    first = k // 2 - h
+                    raw[2 * first + h] = rows[:, :, 0:K_BLOCK]
+                    raw[2 * first + 2 + h] = rows[:, :, K_BLOCK : 2 * K_BLOCK]
+                    r0 = n * ROWS + h * HALF
+                    nc.sync.dma_start(out=rows[:], in_=src[r0 : r0 + HALF, :].rearrange("(p j) c -> p j c", j=2))
+                return
             if k // 2 >= FIRST_WHOLE_BLOCK:
                 if k % 2 == 1:
                     whole = whole_pool.tile([P, 4, K_BLOCK], BF16, name="whole", tag="whole")
@@ -103,11 +113,17 @@ def tile_virtual16bmatmul_kernel(tc, x, weight_upper, weight_lower, out):
 
         def reorder(k):
             reord[k] = reord_pool.tile([P, 2, K_BLOCK // 2], F32, name="reord", tag="reord")
-            words = raw[k].rearrange("p j c -> p (j c)").bitcast(F32)
-            nc.vector.tensor_copy(
-                out=reord[k][:].rearrange("p u (b r) -> p u b r", r=8),
-                in_=words.rearrange("p (b u r) -> p u b r", u=2, r=8),
-            )
+            if k // 2 >= FIRST_ROWS_BLOCK:
+                nc.vector.tensor_copy(
+                    out=reord[k][:].rearrange("p u (j b r) -> p u j b r", j=2, r=8),
+                    in_=raw[k].bitcast(F32).rearrange("p j (b u r) -> p u j b r", u=2, r=8),
+                )
+            else:
+                words = raw[k].rearrange("p j c -> p (j c)").bitcast(F32)
+                nc.vector.tensor_copy(
+                    out=reord[k][:].rearrange("p u (b r) -> p u b r", r=8),
+                    in_=words.rearrange("p (b u r) -> p u b r", u=2, r=8),
+                )
             if k + RAW_BUFS < n_halves:
                 load(k + RAW_BUFS)
 
@@ -170,10 +186,14 @@ def tile_virtual16bmatmul_kernel(tc, x, weight_upper, weight_lower, out):
             if done == PASSES - 1:
                 res = res_pool.tile([P, ROWS], F32, name="res", tag="res")
                 last_n = n == N_TILES - 1
-                if (n == 1 and m % 2 == 1) or (last_n and m % 2 == 0):
-                    nc.vector.tensor_copy(out=res[:], in_=sums)
+                leave = nc.vector.tensor_copy if (n == 1 and m % 2 == 1) or (last_n and m % 2 == 0) else nc.scalar.copy
+                if s >= FIRST_ROWS_BLOCK:
+                    leave(
+                        out=res[:].rearrange("t (a p j) -> t a p j", a=2, j=2),
+                        in_=sums.rearrange("t (a j p) -> t a p j", a=2, j=2),
+                    )
                 else:
-                    nc.scalar.copy(out=res[:], in_=sums)
+                    leave(out=res[:], in_=sums)
                 if n == 0:
                     late_stores.append((m, res))
                 elif last_n and m % 2 == 1:

@@ -251,7 +251,7 @@ def tile_virtual16bmatmul_kernel(tc, x, weight_upper, weight_lower, out):
                 for s in mine:
                     if s < head:
                         continue
-                    transpose(s, True)
+                    transpose(s, s != mine[-1])
                     quantise(s, 0)
                     quantise(s, 1)
                 if n + 1 < N_TILES:

@@ -132,8 +132,9 @@ def tile_virtual16bmatmul_kernel(tc, x, weight_upper, weight_lower, out):
                 grouped_pool.tile([P, ROWS, 2], F32, name="grouped", tag="grouped", align_bytes=64)
                 for g in range(2)
             ]
-            for a in range(2):
-                for g in range(2):
+            order = [(a, g) for g in range(2) for a in range(2)] if s >= len(HEAD_PASSES) else [(a, g) for a in range(2) for g in range(2)]
+            for (a, g) in order:
+                if True:
                     bank = next_bank()
                     for j in range(2):
                         for u in range(2):

@@ -52,7 +52,7 @@ def tile_virtual16bmatmul_kernel(tc, x, weight_upper, weight_lower, out):
         res_pool = ctx.enter_context(tc.tile_pool(name="res_pool", bufs=N_TILES * M_TILES))
         psum = ctx.enter_context(tc.psum_pool(name="psum", bufs=1))
 
-        ident = const.tile([P, P], F32, name="ident")
+        ident = const.tile([P, P], F32, name="ident", align_bytes=256)
         make_identity(nc, ident[:])
         x_codes = const.tile([P, 4, TOKENS], U32, name="x_codes", align_bytes=64)
         x_scales = const.tile([P, 4, TOKENS], U8, name="x_scales", align_bytes=64)
@@ -112,7 +112,7 @@ def tile_virtual16bmatmul_kernel(tc, x, weight_upper, weight_lower, out):
             )
 
         def reorder(k):
-            reord[k] = reord_pool.tile([P, 2, K_BLOCK // 2], F32, name="reord", tag="reord")
+            reord[k] = reord_pool.tile([P, 2, K_BLOCK // 2], F32, name="reord", tag="reord", align_bytes=256)
             if k // 2 >= FIRST_ROWS_BLOCK:
                 nc.vector.tensor_copy(
                     out=reord[k][:].rearrange("p u (j b r) -> p u j b r", j=2, r=8),

@@ -46,13 +46,14 @@ def tile_virtual16bmatmul_kernel(tc, x, weight_upper, weight_lower, out):
         const = ctx.enter_context(tc.tile_pool(name="const", bufs=1))
         raw_pool = ctx.enter_context(tc.tile_pool(name="raw_pool", bufs=2 * FIRST_WHOLE_BLOCK))
         whole_pool = ctx.enter_context(tc.tile_pool(name="whole_pool", bufs=RAW_BUFS // 2))
-        reord_pool = ctx.enter_context(tc.tile_pool(name="reord_pool", bufs=8))
         grouped_pool = ctx.enter_context(tc.tile_pool(name="grouped_pool", bufs=4))
         wq_pool = ctx.enter_context(tc.tile_pool(name="wq_pool", bufs=10))
         res_pool = ctx.enter_context(tc.tile_pool(name="res_pool", bufs=N_TILES * M_TILES))
         psum = ctx.enter_context(tc.psum_pool(name="psum", bufs=1))
+        reord_pool = ctx.enter_context(tc.tile_pool(name="reord_pool", bufs=8))
+        last_const = ctx.enter_context(tc.tile_pool(name="last_const", bufs=1))
 
-        ident = const.tile([P, P], F32, name="ident", align_bytes=256)
+        ident = last_const.tile([P, P], F32, name="ident", align_bytes=256)
         make_identity(nc, ident[:])
         x_codes = const.tile([P, 4, TOKENS], U32, name="x_codes", align_bytes=64)
         x_scales = const.tile([P, 4, TOKENS], U8, name="x_scales", align_bytes=64)

@@ -53,6 +53,8 @@ def tile_virtual16bmatmul_kernel(tc, x, weight_upper, weight_lower, out):
         reord_pool = ctx.enter_context(tc.tile_pool(name="reord_pool", bufs=8))
         last_const = ctx.enter_context(tc.tile_pool(name="last_const", bufs=1))
 
+        pad = wq_pool.tile([P, 16], F32, name="pad", tag="pad", bufs=1, align_bytes=64)
+        nc.gpsimd.memset(pad[:], 0.0)
         ident = last_const.tile([P, P], F32, name="ident", align_bytes=256)
         make_identity(nc, ident[:])
         x_codes = const.tile([P, 4, TOKENS], U32, name="x_codes", align_bytes=64)

@@ -53,7 +53,7 @@ def tile_virtual16bmatmul_kernel(tc, x, weight_upper, weight_lower, out):
         reord_pool = ctx.enter_context(tc.tile_pool(name="reord_pool", bufs=8))
         last_const = ctx.enter_context(tc.tile_pool(name="last_const", bufs=1))
 
-        pad = wq_pool.tile([P, 16], F32, name="pad", tag="pad", bufs=1, align_bytes=64)
+        pad = wq_pool.tile([P, 32], F32, name="pad", tag="pad", bufs=1, align_bytes=64)
         nc.gpsimd.memset(pad[:], 0.0)
         ident = last_const.tile([P, P], F32, name="ident", align_bytes=256)
         make_identity(nc, ident[:])

from contextlib import ExitStack

import concourse.mybir as mybir
from concourse.masks import make_identity

F32 = mybir.dt.float32
BF16 = mybir.dt.bfloat16
U32 = mybir.dt.uint32
U8 = mybir.dt.uint8
E4M3_X4 = mybir.dt.float8_e4m3fn_x4
E5M2_X4 = mybir.dt.float8_e5m2_x4

TOKENS, D_IN, D_OUT = 512, 2048, 2048
FLOPS = 2 * 2 * TOKENS * D_IN * D_OUT

P = 128
K_PASS = 512
ROWS = 512
HALF = 256
K_BLOCK = 2 * K_PASS
N_TILES = D_OUT // ROWS
M_TILES = TOKENS // P
PASSES = 2 * D_IN // K_PASS

RAW_BUFS = 16
FIRST_WHOLE_BLOCK = 6
FIRST_ROWS_BLOCK = 10
HEAD_PASSES = (0, 0, 1, 1, 2, 2, 2)
FIRST_SWEEP = 3
KEEP_WARM = 3


def tile_virtual16bmatmul_kernel(tc, x, weight_upper, weight_lower, out):
    nc = tc.nc
    x_flat = x.flatten_outer_dims()
    out_flat = out.flatten_outer_dims()

    blocks = [(x_flat, 0, 0), (weight_upper, 0, 0), (x_flat, 0, 1), (weight_upper, 0, 1)]
    blocks += [(weight_lower, 0, 0), (weight_lower, 0, 1)]
    for n in range(1, N_TILES):
        blocks += [(weight_upper, n, 0), (weight_upper, n, 1), (weight_lower, n, 0), (weight_lower, n, 1)]
    n_halves = 2 * len(blocks)
    head = len(HEAD_PASSES)

    with ExitStack() as ctx:
        const = ctx.enter_context(tc.tile_pool(name="const", bufs=1))
        raw_pool = ctx.enter_context(tc.tile_pool(name="raw_pool", bufs=2 * FIRST_WHOLE_BLOCK))
        whole_pool = ctx.enter_context(tc.tile_pool(name="whole_pool", bufs=RAW_BUFS // 2))
        grouped_pool = ctx.enter_context(tc.tile_pool(name="grouped_pool", bufs=4))
        wq_pool = ctx.enter_context(tc.tile_pool(name="wq_pool", bufs=10))
        res_pool = ctx.enter_context(tc.tile_pool(name="res_pool", bufs=N_TILES * M_TILES))
        psum = ctx.enter_context(tc.psum_pool(name="psum", bufs=1))
        reord_pool = ctx.enter_context(tc.tile_pool(name="reord_pool", bufs=8))
        last_const = ctx.enter_context(tc.tile_pool(name="last_const", bufs=1))

        pad = wq_pool.tile([P, 32], F32, name="pad", tag="pad", bufs=1, align_bytes=64)
        nc.gpsimd.memset(pad[:], 0.0)
        ident = last_const.tile([P, P], F32, name="ident", align_bytes=256)
        make_identity(nc, ident[:])
        x_codes = const.tile([P, 4, TOKENS], U32, name="x_codes", align_bytes=64)
        x_scales = const.tile([P, 4, TOKENS], U8, name="x_scales", align_bytes=64)
        warm_in = const.tile([P, 1], F32, name="warm_in")
        warm_out = const.tile([P, 1], F32, name="warm_out")
        zero_l = const.tile([P, P], BF16, name="zero_l")
        zero_r = const.tile([P, ROWS], BF16, name="zero_r")
        warm_banks = {}

        raw = {}
        reord = {}
        grouped = {}
        w_quantised = {}
        acc = {}
        passes_done = {}
        rotation = {"banks": [4, 5, 6, 7], "taken": 0}
        late_stores = []

        def bank_tile(b):
            return psum.tile([P, 2, HALF], F32, name="bank%d" % b, tag="bank%d" % b)

        def next_bank():
            banks = rotation["banks"]
            b = banks[rotation["taken"] % len(banks)]
            rotation["taken"] += 1
            return bank_tile(b)

        def load(k):
            src, n, h = blocks[k // 2]
            if k // 2 >= FIRST_ROWS_BLOCK:
                if k % 2 == 1:
                    rows = whole_pool.tile([P, 2, D_IN], BF16, name="whole", tag="whole")
                    first = k // 2 - h
                    raw[2 * first + h] = rows[:, :, 0:K_BLOCK]
                    raw[2 * first + 2 + h] = rows[:, :, K_BLOCK : 2 * K_BLOCK]
                    r0 = n * ROWS + h * HALF
                    nc.sync.dma_start(out=rows[:], in_=src[r0 : r0 + HALF, :].rearrange("(p j) c -> p j c", j=2))
                return
            if k // 2 >= FIRST_WHOLE_BLOCK:
                if k % 2 == 1:
                    whole = whole_pool.tile([P, 4, K_BLOCK], BF16, name="whole", tag="whole")
                    raw[k - 1] = whole[:, 0:2, :]
                    raw[k] = whole[:, 2:4, :]
                    nc.sync.dma_start(
                        out=whole[:],
                        in_=src[n * ROWS : (n + 1) * ROWS, h * K_BLOCK : (h + 1) * K_BLOCK].rearrange(
                            "(j p) c -> p j c", p=P
                        ),
                    )
                return
            r0 = n * ROWS + (k % 2) * HALF
            half = raw_pool.tile([P, 2, K_BLOCK], BF16, name="raw", tag="raw")
            raw[k] = half[:]
            nc.sync.dma_start(
                out=half[:],
                in_=src[r0 : r0 + HALF, h * K_BLOCK : (h + 1) * K_BLOCK].rearrange("(j p) c -> p j c", p=P),
            )

        def reorder(k):
            reord[k] = reord_pool.tile([P, 2, K_BLOCK // 2], F32, name="reord", tag="reord", align_bytes=256)
            if k // 2 >= FIRST_ROWS_BLOCK:
                nc.vector.tensor_copy(
                    out=reord[k][:].rearrange("p u (j b r) -> p u j b r", j=2, r=8),
                    in_=raw[k].bitcast(F32).rearrange("p j (b u r) -> p u j b r", u=2, r=8),
                )
            else:
                words = raw[k].rearrange("p j c -> p (j c)").bitcast(F32)
                nc.vector.tensor_copy(
                    out=reord[k][:].rearrange("p u (b r) -> p u b r", r=8),
                    in_=words.rearrange("p (b u r) -> p u b r", u=2, r=8),
                )
            if k + RAW_BUFS < n_halves:
                load(k + RAW_BUFS)

        def transpose(s, vector_helps):
            grouped[s] = [
                grouped_pool.tile([P, ROWS, 2], F32, name="grouped", tag="grouped", align_bytes=64)
                for g in range(2)
            ]
            order = [(a, g) for g in range(2) for a in range(2)] if s >= len(HEAD_PASSES) else [(a, g) for a in range(2) for g in range(2)]
            for (a, g) in order:
                if True:
                    bank = next_bank()
                    for j in range(2):
                        for u in range(2):
                            c0 = (2 * j + g) * P
                            nc.tensor.transpose(
                                out=bank[:, u, j * P : (j + 1) * P],
                                in_=reord[2 * s + a][:, u, c0 : c0 + P],
                                identity=ident[:],
                            )
                    empty = nc.vector.tensor_copy if (vector_helps and a == 1 and g == 1) else nc.scalar.copy
                    empty(
                        out=grouped[s][g][:, a * HALF : (a + 1) * HALF, :],
                        in_=bank[:].rearrange("p u r -> p r u"),
                    )

        def quantise(s, g):
            src, n, h = blocks[s]
            values = grouped[s][g][:].rearrange("p r u -> p (r u)").bitcast(BF16)
            if src is x_flat:
                nc.vector.quantize_mx(
                    out=x_codes[:, 2 * h + g, :].bitcast(E5M2_X4), scales=x_scales[:, 2 * h + g, :], in_=values
                )
            else:
                w_codes = wq_pool.tile([P, ROWS], U32, name="w_codes", tag="w_codes", align_bytes=64)
                w_scales = wq_pool.tile([P, ROWS], U8, name="w_scales", tag="w_scales", align_bytes=64)
                w_quantised[(s, g)] = (w_codes, w_scales)
                nc.vector.quantize_mx(out=w_codes[:].bitcast(E4M3_X4), scales=w_scales[:], in_=values)

        def one_pass(s, g, m):
            src, n, h = blocks[s]
            done = passes_done.get((n, m), 0)
            passes_done[(n, m)] = done + 1
            if done == 0:
                if n == 0:
                    acc[m] = warm_banks[m] if m in warm_banks else bank_tile(m)
                else:
                    acc[m] = next_bank()
            w_codes, w_scales = w_quantised[(s, g)]
            tokens = slice(m * P, (m + 1) * P)
            sums = acc[m][:].rearrange("p a b -> p (a b)")
            nc.tensor.matmul_mx(
                out=sums,
                lhsT=x_codes[:, 2 * h + g, tokens].bitcast(E5M2_X4),
                lhsT_scale=x_scales[:, 2 * h + g, tokens],
                rhs=w_codes[:].bitcast(E4M3_X4),
                rhs_scale=w_scales[:],
                start=(done == 0),
                stop=(done == PASSES - 1),
            )
            if done == PASSES - 1:
                res = res_pool.tile([P, ROWS], F32, name="res", tag="res")
                last_n = n == N_TILES - 1
                leave = nc.vector.tensor_copy if (n == 1 and m % 2 == 1) or (last_n and m % 2 == 0) else nc.scalar.copy
                if s >= FIRST_ROWS_BLOCK:
                    leave(
                        out=res[:].rearrange("t (a p j) -> t a p j", a=2, j=2),
                        in_=sums.rearrange("t (a j p) -> t a p j", a=2, j=2),
                    )
                else:
                    leave(out=res[:], in_=sums)
                if n == 0:
                    late_stores.append((m, res))
                elif last_n and m % 2 == 1:
                    nc.scalar.dma_start(out=out_flat[m * P : (m + 1) * P, n * ROWS : (n + 1) * ROWS], in_=res[:])
                else:
                    nc.sync.dma_start(out=out_flat[m * P : (m + 1) * P, n * ROWS : (n + 1) * ROWS], in_=res[:])

        with tc.manual_schedule():
            nc.vector.memset(warm_in[:], 0.0)
            nc.vector.memset(zero_l[:], 0.0)
            nc.vector.memset(zero_r[:], 0.0)
            nc.scalar.copy(out=warm_out[:], in_=warm_in[:])
            for k in range(RAW_BUFS):
                load(k)
            reorder(0)
            reorder(1)

            head_passes = [(b, g) for b in range(head - 1) if blocks[b][0] is not x_flat for g in range(2)]
            sent = 0
            for s in range(head):
                transpose(s, False)
                if s == 1:
                    for i in range(KEEP_WARM):
                        warm_banks[i] = bank_tile(i)
                        nc.tensor.matmul(
                            out=warm_banks[i][:].rearrange("p a b -> p (a b)"),
                            lhsT=zero_l[:],
                            rhs=zero_r[:],
                            start=True,
                            stop=True,
                        )
                reorder(2 * s + 2)
                reorder(2 * s + 3)
                quantise(s, 0)
                quantise(s, 1)
                now = head_passes[sent : sent + HEAD_PASSES[s]]
                sent += HEAD_PASSES[s]
                if sent < len(head_passes):
                    for (b, g) in now:
                        for m in range(M_TILES):
                            one_pass(b, g, m)
                else:
                    for m in range(M_TILES):
                        for (b, g) in now:
                            one_pass(b, g, m)

            rotation["banks"] = [4, 5, 6, 7, 0, 1, 2, 3]
            rotation["taken"] = 0
            for k in range(2 * head + 2, 2 * head + 6):
                reorder(k)
            for (m, res) in late_stores:
                nc.sync.dma_start(out=out_flat[m * P : (m + 1) * P, 0:ROWS], in_=res[:])
            for n in range(1, N_TILES):
                mine = [4 * n + 2 + i for i in range(4)]
                for s in mine:
                    if s < head:
                        continue
                    transpose(s, s != mine[-1])
                    quantise(s, 0)
                    quantise(s, 1)
                if n + 1 < N_TILES:
                    for k in range(2 * (mine[0] + 4), 2 * (mine[0] + 8)):
                        reorder(k)
                pieces = [(s, g) for s in mine for g in range(2)]
                for m in range(M_TILES):
                    for (s, g) in pieces[: FIRST_SWEEP + m]:
                        one_pass(s, g, m)
                for m in range(M_TILES):
                    for (s, g) in pieces[FIRST_SWEEP + m :]:
                        one_pass(s, g, m)
